import numpy as np
import ml_dtypes


def mxq(x, axis, fmt="e4m3"):
    dtype, down = {"e4m3": (ml_dtypes.float8_e4m3fn, 7), "e5m2": (ml_dtypes.float8_e5m2, 14)}[fmt]
    v = np.moveaxis(np.asarray(x, np.float32).astype(ml_dtypes.bfloat16).astype(np.float64), axis, -1)
    blocks = v.reshape(v.shape[:-1] + (-1, 32))
    amax = np.abs(blocks).max(-1, keepdims=True)
    byte = np.maximum(np.where(amax > 0, np.frexp(amax)[1] - 1 + 127, 0) - down, 1)
    scale = np.exp2(byte - 127.0)
    codes = (blocks / scale).astype(np.float32).astype(dtype).astype(np.float64)
    return np.moveaxis((codes * scale).reshape(v.shape), -1, axis)


WIDE = False


def mx_kscale(k):
    if not WIDE:
        return np.ones(k)
    levels = np.array([10, -10, 5, -5, 0])
    a = np.random.permutation(np.resize(levels, k // 512 * 4)).reshape(k // 512, 4)
    idx = np.arange(k)
    return np.exp2(a[idx // 512, idx % 128 // 32])


BF16 = ml_dtypes.bfloat16


def bf(x):
    return np.asarray(x, np.float32).astype(BF16)


def f64(x):
    return np.asarray(x).astype(np.float64)


N, C, H, W, B = 1024, 64, 4, 4, 128
D = C * H * W
EPS = 1e-8
TINY = 1e-16


def setup_inputs():
    s = mx_kscale(D)
    g = np.sqrt(np.mean(s * s) * np.mean(1.0 / (s * s)))
    key = np.random.standard_normal((B, D)) * (0.5 + np.random.random((B, 1)))
    memory = np.random.standard_normal((N, D)) * (0.5 + np.random.random((N, 1))) * 3.0
    strength = np.sqrt(D) * g * (0.5 + 0.5 * np.random.random((B, 1)))
    sharpen = 1.0 + np.random.random((B, 1))
    return {"memory": bf((memory / s).reshape(N, C, H, W)), "key": bf(key * s), "strength": bf(strength), "sharpen": bf(sharpen)}


def reference(memory, key, strength, sharpen):
    mem_flat = f64(memory).reshape(N, D)
    k = f64(key)
    key_norm = np.sqrt((k * k).sum(-1, keepdims=True))
    mem_norm = np.sqrt((mem_flat * mem_flat).sum(-1))
    dot = mxq(k, 1, "e4m3") @ mxq(mem_flat, 1, "e4m3").T
    sim = dot / (np.maximum(key_norm, EPS) * np.maximum(mem_norm, EPS)[None, :])
    z = f64(strength) * sim
    e = np.exp(z - z.max(1, keepdims=True))
    w = e / e.sum(1, keepdims=True)
    w = w ** f64(sharpen)
    return w / (w.sum(1, keepdims=True) + TINY)

@@ -1,0 +1,275 @@
+from contextlib import ExitStack
+
+import concourse.masks as masks
+import concourse.mybir as mybir
+
+F32 = mybir.dt.float32
+BF16 = mybir.dt.bfloat16
+U32 = mybir.dt.uint32
+U8 = mybir.dt.uint8
+FP8X4 = mybir.dt.float8_e4m3fn_x4
+ALU = mybir.AluOpType
+ACT = mybir.ActivationFunctionType
+AXIS = mybir.AxisListType
+
+P = 128
+SLOTS = 1024
+FEATURES = 1024
+KEYS = 128
+PACK = 4
+K_PASS = P * PACK
+PASSES = FEATURES // K_PASS
+PAIRS = FEATURES // 2
+PAIR_BLOCKS = PAIRS // P
+HALVES = PAIR_BLOCKS // PASSES
+TILE_WORDS = PASSES * P
+SLOT_TILES = SLOTS // P
+TILES_PER_ROUND = 2
+ROUNDS = SLOT_TILES // TILES_PER_ROUND
+BANK = 512
+TILES_PER_BANK = BANK // P
+OUT_BANKS = SLOTS // BANK
+EPS = 1e-8
+TINY = 1e-16
+
+FLOPS = 2 * KEYS * SLOTS * FEATURES
+
+
+def transpose_pairs(nc, bank, rows, identity):
+    pairs = rows.bitcast(F32)
+    for j in range(PAIR_BLOCKS):
+        nc.tensor.transpose(bank[:, j, :], pairs[:, j * P : (j + 1) * P], identity)
+
+
+def regroup(nc, grouped, bank):
+    nc.vector.tensor_copy(
+        out=grouped.bitcast(F32).rearrange("p (g r u) -> p g r u", g=PASSES, u=HALVES),
+        in_=bank.rearrange("p (g u) r -> p g r u", u=HALVES),
+    )
+
+
+def tile_memory_pa_s_kernel(tc, memory, key, strength, sharpen, out):
+    nc = tc.nc
+    mem = memory.rearrange("n c h w -> n (c h w)")
+    with ExitStack() as ctx:
+        keep = ctx.enter_context(tc.tile_pool(name="keep", bufs=1))
+        stage = ctx.enter_context(tc.tile_pool(name="stage", bufs=2))
+        pair_banks = ctx.enter_context(tc.psum_pool(name="pair_banks", bufs=4))
+        dot_banks = ctx.enter_context(tc.psum_pool(name="dot_banks", bufs=2))
+        sim_banks = ctx.enter_context(tc.psum_pool(name="sim_banks", bufs=1))
+        ctx.enter_context(tc.manual_schedule())
+
+        key_rows = keep.tile([P, FEATURES], BF16)
+        nc.sync.dma_start(out=key_rows[:], in_=key)
+        mem_rows = []
+        for t in range(SLOT_TILES):
+            rows = keep.tile([P, FEATURES], BF16, name="mem_rows%d" % t)
+            nc.sync.dma_start(out=rows[:], in_=mem[t * P : (t + 1) * P, :])
+            mem_rows.append(rows)
+
+        identity = keep.tile([P, P], F32)
+        masks.make_identity(nc, identity[:])
+        strength_col = keep.tile([P, 1], BF16)
+        nc.gpsimd.dma_start(out=strength_col[:], in_=strength)
+        sharpen_col = keep.tile([P, 1], BF16)
+        nc.gpsimd.dma_start(out=sharpen_col[:], in_=sharpen)
+        minus_half = keep.tile([P, SLOT_TILES], F32)
+        nc.vector.memset(minus_half[:], -0.5)
+        zero_col = keep.tile([P, 1], F32)
+        nc.vector.memset(zero_col[:], 0.0)
+        warm_col = keep.tile([P, 1], F32)
+        nc.scalar.activation(out=warm_col[:], in_=zero_col[:], func=ACT.Exp)
+
+        squares = keep.tile([P, 1 + SLOT_TILES, FEATURES], BF16)
+        key_sumsq = keep.tile([P, 1], F32)
+        nc.scalar.activation(
+            out=squares[:, SLOT_TILES, :], in_=key_rows[:], func=ACT.Square, accum_out=key_sumsq[:]
+        )
+        key_clamped = keep.tile([P, 1], F32)
+        nc.gpsimd.tensor_scalar(
+            out=key_clamped[:], in0=key_sumsq[:], scalar1=EPS * EPS, scalar2=None, op0=ALU.max
+        )
+        key_inv_norm = keep.tile([P, 1], F32)
+        nc.gpsimd.tensor_tensor(
+            out=key_inv_norm[:], in0=key_clamped[:], in1=minus_half[:, 0:1], op=ALU.pow
+        )
+        gain = keep.tile([P, 1], F32)
+        nc.gpsimd.tensor_tensor(out=gain[:], in0=key_inv_norm[:], in1=strength_col[:], op=ALU.mult)
+        sharpen_f32 = keep.tile([P, 1], F32)
+        nc.gpsimd.tensor_copy(out=sharpen_f32[:], in_=sharpen_col[:])
+
+        mem_sumsq = keep.tile([P, SLOT_TILES], F32)
+        mem_clamped = keep.tile([P, SLOT_TILES], F32)
+        mem_inv_norm = keep.tile([P, SLOT_TILES], F32)
+        for r in range(ROUNDS):
+            tiles = slice(r * TILES_PER_ROUND, (r + 1) * TILES_PER_ROUND)
+            for t in range(r * TILES_PER_ROUND, (r + 1) * TILES_PER_ROUND):
+                nc.scalar.activation(
+                    out=squares[:, t, :],
+                    in_=mem_rows[t][:],
+                    func=ACT.Square,
+                    accum_out=mem_sumsq[:, t : t + 1],
+                )
+            nc.gpsimd.tensor_scalar(
+                out=mem_clamped[:, tiles],
+                in0=mem_sumsq[:, tiles],
+                scalar1=EPS * EPS,
+                scalar2=None,
+                op0=ALU.max,
+            )
+            nc.gpsimd.tensor_tensor(
+                out=mem_inv_norm[:, tiles],
+                in0=mem_clamped[:, tiles],
+                in1=minus_half[:, tiles],
+                op=ALU.pow,
+            )
+
+        banks_of = {}
+        grouped_of = {}
+        codes_of = {}
+        scales_of = {}
+        dot_of = {}
+        sim_t_of = {}
+        sim = [sim_banks.tile([P, BANK], F32, name="sim%d" % h) for h in range(OUT_BANKS)]
+
+        def transpose_round(r):
+            banks_of[r] = []
+            for i in range(TILES_PER_ROUND):
+                bank = pair_banks.tile([P, PAIR_BLOCKS, P], F32, name="pair_bank")
+                transpose_pairs(nc, bank, mem_rows[r * TILES_PER_ROUND + i][:], identity[:])
+                banks_of[r].append(bank)
+
+        def regroup_round(r):
+            grouped = stage.tile(
+                [P, TILES_PER_ROUND, TILE_WORDS * PACK], BF16, name="grouped", align_bytes=64
+            )
+            for i in range(TILES_PER_ROUND):
+                regroup(nc, grouped[:, i, :], banks_of[r][i][:])
+            grouped_of[r] = grouped
+
+        def quantise_round(r):
+            codes = stage.tile([P, TILES_PER_ROUND * TILE_WORDS], U32, name="codes", align_bytes=64)
+            scales = stage.tile([P, TILES_PER_ROUND * TILE_WORDS], U8, name="scales", align_bytes=64)
+            nc.vector.quantize_mx(
+                out=codes[:].bitcast(FP8X4),
+                scales=scales[:],
+                in_=grouped_of[r][:].rearrange("p i c -> p (i c)"),
+            )
+            codes_of[r] = codes
+            scales_of[r] = scales
+
+        def multiply_round(r):
+            dot = dot_banks.tile([P, TILES_PER_ROUND, KEYS], F32, name="dot")
+            for i in range(TILES_PER_ROUND):
+                for g in range(PASSES):
+                    slot_cols = slice((i * PASSES + g) * P, (i * PASSES + g + 1) * P)
+                    key_cols = slice(g * KEYS, (g + 1) * KEYS)
+                    nc.tensor.matmul_mx(
+                        out=dot[:, i, :],
+                        lhsT=codes_of[r][:, slot_cols].bitcast(FP8X4),
+                        lhsT_scale=scales_of[r][:, slot_cols],
+                        rhs=key_codes[:, key_cols].bitcast(FP8X4),
+                        rhs_scale=key_scales[:, key_cols],
+                        start=(g == 0),
+                        stop=(g == PASSES - 1),
+                    )
+            dot_of[r] = dot
+
+        def normalise_round(r):
+            tiles = slice(r * TILES_PER_ROUND, (r + 1) * TILES_PER_ROUND)
+            sim_t = stage.tile([P, TILES_PER_ROUND, KEYS], F32, name="sim_t")
+            nc.vector.tensor_tensor(
+                out=sim_t[:],
+                in0=dot_of[r][:],
+                in1=mem_inv_norm[:, tiles].unsqueeze(2).to_broadcast([P, TILES_PER_ROUND, KEYS]),
+                op=ALU.mult,
+            )
+            sim_t_of[r] = sim_t
+
+        def transpose_back_round(r):
+            for i in range(TILES_PER_ROUND):
+                t = r * TILES_PER_ROUND + i
+                cols = slice((t % TILES_PER_BANK) * P, (t % TILES_PER_BANK + 1) * P)
+                nc.tensor.transpose(sim[t // TILES_PER_BANK][:, cols], sim_t_of[r][:, i, :], identity[:])
+
+        z = keep.tile([P, SLOTS], F32)
+        z_max = keep.tile([P, OUT_BANKS], F32)
+
+        def scale_bank(h):
+            nc.vector.tensor_scalar(
+                out=z[:, h * BANK : (h + 1) * BANK],
+                in0=sim[h][:],
+                scalar1=gain[:, 0:1],
+                scalar2=None,
+                op0=ALU.mult,
+                op1=ALU.max,
+                accum_out=z_max[:, h : h + 1],
+            )
+
+        key_bank = pair_banks.tile([P, PAIR_BLOCKS, P], F32, name="pair_bank")
+        transpose_pairs(nc, key_bank, key_rows[:], identity[:])
+        key_grouped = keep.tile([P, TILE_WORDS * PACK], BF16, align_bytes=64)
+        regroup(nc, key_grouped[:], key_bank[:])
+        transpose_round(0)
+        regroup_round(0)
+        key_codes = keep.tile([P, TILE_WORDS], U32, align_bytes=64)
+        key_scales = keep.tile([P, TILE_WORDS], U8, align_bytes=64)
+        nc.vector.quantize_mx(
+            out=key_codes[:].bitcast(FP8X4), scales=key_scales[:], in_=key_grouped[:]
+        )
+        transpose_round(1)
+
+        rounds_per_bank = TILES_PER_BANK // TILES_PER_ROUND
+        for s in range(ROUNDS + 2):
+            if s + 2 < ROUNDS:
+                transpose_round(s + 2)
+            if s + 1 < ROUNDS:
+                regroup_round(s + 1)
+            if s < ROUNDS:
+                quantise_round(s)
+                multiply_round(s)
+            if 1 <= s <= ROUNDS:
+                normalise_round(s - 1)
+                transpose_back_round(s - 1)
+            if s >= 2 and (s - 1) % rounds_per_bank == 0:
+                scale_bank((s - 2) // rounds_per_bank)
+
+        neg_max = keep.tile([P, 1], F32)
+        nc.vector.tensor_reduce(out=neg_max[:], in_=z_max[:], axis=AXIS.X, op=ALU.max, negate=True)
+        e_unread = keep.tile([P, SLOTS], BF16)
+        e_sum = keep.tile([P, 1], F32)
+        nc.scalar.activation(
+            out=e_unread[:], in_=z[:], func=ACT.Exp, bias=neg_max[:, 0:1], scale=1.0, accum_out=e_sum[:]
+        )
+        neg_max_sharp = keep.tile([P, 1], F32)
+        nc.vector.tensor_tensor(out=neg_max_sharp[:], in0=neg_max[:], in1=sharpen_f32[:], op=ALU.mult)
+        v = keep.tile([P, SLOTS], F32)
+        v_sum = keep.tile([P, 1], F32)
+        nc.scalar.activation(
+            out=v[:],
+            in_=z[:],
+            func=ACT.Exp,
+            bias=neg_max_sharp[:, 0:1],
+            scale=sharpen_f32[:, 0:1],
+            accum_out=v_sum[:],
+        )
+        e_sum_sharp = keep.tile([P, 1], F32)
+        nc.gpsimd.tensor_tensor(out=e_sum_sharp[:], in0=e_sum[:], in1=sharpen_f32[:], op=ALU.pow)
+        denominator = keep.tile([P, 1], F32)
+        nc.vector.tensor_scalar(
+            out=denominator[:],
+            in0=e_sum_sharp[:],
+            scalar1=TINY,
+            scalar2=v_sum[:, 0:1],
+            op0=ALU.mult,
+            op1=ALU.add,
+        )
+        inv_denominator = keep.tile([P, 1], F32)
+        nc.vector.reciprocal(out=inv_denominator[:], in_=denominator[:])
+        w = keep.tile([P, SLOTS], F32)
+        for h in range(OUT_BANKS):
+            cols = slice(h * BANK, (h + 1) * BANK)
+            nc.vector.tensor_scalar(
+                out=w[:, cols], in0=v[:, cols], scalar1=inv_denominator[:, 0:1], scalar2=None, op0=ALU.mult
+            )
+            nc.sync.dma_start(out=out[:, cols], in_=w[:, cols])

@@ -73,33 +73,34 @@ def tile_memory_pa_s_kernel(tc, memory, key, strength, sharpen, out):
         nc.gpsimd.dma_start(out=strength_col[:], in_=strength)
         sharpen_col = keep.tile([P, 1], BF16)
         nc.gpsimd.dma_start(out=sharpen_col[:], in_=sharpen)
-        minus_half = keep.tile([P, SLOT_TILES], F32)
-        nc.vector.memset(minus_half[:], -0.5)
         zero_col = keep.tile([P, 1], F32)
         nc.vector.memset(zero_col[:], 0.0)
-        warm_col = keep.tile([P, 1], F32)
-        nc.scalar.activation(out=warm_col[:], in_=zero_col[:], func=ACT.Exp)
+        one_col = keep.tile([P, 1], F32)
+        nc.vector.memset(one_col[:], 1.0)
+        warm_norms = keep.tile([P, 1], F32)
+        nc.scalar.activation(out=warm_norms[:], in_=one_col[:], func=ACT.Abs_reciprocal_sqrt)
+
+        def invert_norms(inv_norm, excess, sumsq):
+            nc.scalar.activation(out=excess, in_=sumsq, func=ACT.Relu, bias=-EPS * EPS)
+            nc.scalar.activation(
+                out=inv_norm, in_=excess, func=ACT.Abs_reciprocal_sqrt, bias=EPS * EPS
+            )
 
         squares = keep.tile([P, 1 + SLOT_TILES, FEATURES], BF16)
         key_sumsq = keep.tile([P, 1], F32)
         nc.scalar.activation(
             out=squares[:, SLOT_TILES, :], in_=key_rows[:], func=ACT.Square, accum_out=key_sumsq[:]
         )
-        key_clamped = keep.tile([P, 1], F32)
-        nc.gpsimd.tensor_scalar(
-            out=key_clamped[:], in0=key_sumsq[:], scalar1=EPS * EPS, scalar2=None, op0=ALU.max
-        )
+        key_excess = keep.tile([P, 1], F32)
         key_inv_norm = keep.tile([P, 1], F32)
-        nc.gpsimd.tensor_tensor(
-            out=key_inv_norm[:], in0=key_clamped[:], in1=minus_half[:, 0:1], op=ALU.pow
-        )
+        invert_norms(key_inv_norm[:], key_excess[:], key_sumsq[:])
         gain = keep.tile([P, 1], F32)
         nc.gpsimd.tensor_tensor(out=gain[:], in0=key_inv_norm[:], in1=strength_col[:], op=ALU.mult)
         sharpen_f32 = keep.tile([P, 1], F32)
         nc.gpsimd.tensor_copy(out=sharpen_f32[:], in_=sharpen_col[:])
 
         mem_sumsq = keep.tile([P, SLOT_TILES], F32)
-        mem_clamped = keep.tile([P, SLOT_TILES], F32)
+        mem_excess = keep.tile([P, SLOT_TILES], F32)
         mem_inv_norm = keep.tile([P, SLOT_TILES], F32)
         for r in range(ROUNDS):
             tiles = slice(r * TILES_PER_ROUND, (r + 1) * TILES_PER_ROUND)
@@ -110,19 +111,9 @@ def tile_memory_pa_s_kernel(tc, memory, key, strength, sharpen, out):
                     func=ACT.Square,
                     accum_out=mem_sumsq[:, t : t + 1],
                 )
-            nc.gpsimd.tensor_scalar(
-                out=mem_clamped[:, tiles],
-                in0=mem_sumsq[:, tiles],
-                scalar1=EPS * EPS,
-                scalar2=None,
-                op0=ALU.max,
-            )
-            nc.gpsimd.tensor_tensor(
-                out=mem_inv_norm[:, tiles],
-                in0=mem_clamped[:, tiles],
-                in1=minus_half[:, tiles],
-                op=ALU.pow,
-            )
+            invert_norms(mem_inv_norm[:, tiles], mem_excess[:, tiles], mem_sumsq[:, tiles])
+        warm_exp = keep.tile([P, 1], F32)
+        nc.scalar.activation(out=warm_exp[:], in_=zero_col[:], func=ACT.Exp)
 
         banks_of = {}
         grouped_of = {}

@@ -10,7 +10,6 @@ U8 = mybir.dt.uint8
 FP8X4 = mybir.dt.float8_e4m3fn_x4
 ALU = mybir.AluOpType
 ACT = mybir.ActivationFunctionType
-AXIS = mybir.AxisListType
 
 P = 128
 SLOTS = 1024
@@ -73,34 +72,43 @@ def tile_memory_pa_s_kernel(tc, memory, key, strength, sharpen, out):
         nc.gpsimd.dma_start(out=strength_col[:], in_=strength)
         sharpen_col = keep.tile([P, 1], BF16)
         nc.gpsimd.dma_start(out=sharpen_col[:], in_=sharpen)
+        minus_half = keep.tile([P, SLOT_TILES], F32)
+        nc.vector.memset(minus_half[:], -0.5)
         zero_col = keep.tile([P, 1], F32)
         nc.vector.memset(zero_col[:], 0.0)
-        one_col = keep.tile([P, 1], F32)
-        nc.vector.memset(one_col[:], 1.0)
-        warm_norms = keep.tile([P, 1], F32)
-        nc.scalar.activation(out=warm_norms[:], in_=one_col[:], func=ACT.Abs_reciprocal_sqrt)
-
-        def invert_norms(inv_norm, excess, sumsq):
-            nc.scalar.activation(out=excess, in_=sumsq, func=ACT.Relu, bias=-EPS * EPS)
-            nc.scalar.activation(
-                out=inv_norm, in_=excess, func=ACT.Abs_reciprocal_sqrt, bias=EPS * EPS
-            )
+        warm_col = keep.tile([P, 1], F32)
+        nc.scalar.activation(out=warm_col[:], in_=zero_col[:], func=ACT.Exp)
 
         squares = keep.tile([P, 1 + SLOT_TILES, FEATURES], BF16)
         key_sumsq = keep.tile([P, 1], F32)
         nc.scalar.activation(
             out=squares[:, SLOT_TILES, :], in_=key_rows[:], func=ACT.Square, accum_out=key_sumsq[:]
         )
-        key_excess = keep.tile([P, 1], F32)
         key_inv_norm = keep.tile([P, 1], F32)
-        invert_norms(key_inv_norm[:], key_excess[:], key_sumsq[:])
-        gain = keep.tile([P, 1], F32)
-        nc.gpsimd.tensor_tensor(out=gain[:], in0=key_inv_norm[:], in1=strength_col[:], op=ALU.mult)
+        nc.gpsimd.tensor_tensor(
+            out=key_inv_norm[:], in0=key_sumsq[:], in1=minus_half[:, 0:1], op=ALU.pow
+        )
+        key_inv_clamped = keep.tile([P, 1], F32)
+        nc.gpsimd.tensor_scalar(
+            out=key_inv_clamped[:],
+            in0=key_inv_norm[:],
+            scalar1=1.0 / EPS,
+            scalar2=-1.0,
+            op0=ALU.min,
+            op1=ALU.mult,
+        )
+        neg_gain = keep.tile([P, 1], F32)
+        nc.gpsimd.tensor_tensor(
+            out=neg_gain[:], in0=key_inv_clamped[:], in1=strength_col[:], op=ALU.mult
+        )
         sharpen_f32 = keep.tile([P, 1], F32)
         nc.gpsimd.tensor_copy(out=sharpen_f32[:], in_=sharpen_col[:])
+        neg_sharpen = keep.tile([P, 1], F32)
+        nc.gpsimd.tensor_scalar(
+            out=neg_sharpen[:], in0=sharpen_col[:], scalar1=-1.0, scalar2=None, op0=ALU.mult
+        )
 
         mem_sumsq = keep.tile([P, SLOT_TILES], F32)
-        mem_excess = keep.tile([P, SLOT_TILES], F32)
         mem_inv_norm = keep.tile([P, SLOT_TILES], F32)
         for r in range(ROUNDS):
             tiles = slice(r * TILES_PER_ROUND, (r + 1) * TILES_PER_ROUND)
@@ -111,9 +119,12 @@ def tile_memory_pa_s_kernel(tc, memory, key, strength, sharpen, out):
                     func=ACT.Square,
                     accum_out=mem_sumsq[:, t : t + 1],
                 )
-            invert_norms(mem_inv_norm[:, tiles], mem_excess[:, tiles], mem_sumsq[:, tiles])
-        warm_exp = keep.tile([P, 1], F32)
-        nc.scalar.activation(out=warm_exp[:], in_=zero_col[:], func=ACT.Exp)
+            nc.gpsimd.tensor_tensor(
+                out=mem_inv_norm[:, tiles],
+                in0=mem_sumsq[:, tiles],
+                in1=minus_half[:, tiles],
+                op=ALU.pow,
+            )
 
         banks_of = {}
         grouped_of = {}
@@ -169,11 +180,13 @@ def tile_memory_pa_s_kernel(tc, memory, key, strength, sharpen, out):
         def normalise_round(r):
             tiles = slice(r * TILES_PER_ROUND, (r + 1) * TILES_PER_ROUND)
             sim_t = stage.tile([P, TILES_PER_ROUND, KEYS], F32, name="sim_t")
-            nc.vector.tensor_tensor(
+            nc.vector.scalar_tensor_tensor(
                 out=sim_t[:],
-                in0=dot_of[r][:],
-                in1=mem_inv_norm[:, tiles].unsqueeze(2).to_broadcast([P, TILES_PER_ROUND, KEYS]),
-                op=ALU.mult,
+                in0=mem_inv_norm[:, tiles].unsqueeze(2).to_broadcast([P, TILES_PER_ROUND, KEYS]),
+                scalar=1.0 / EPS,
+                in1=dot_of[r][:],
+                op0=ALU.min,
+                op1=ALU.mult,
             )
             sim_t_of[r] = sim_t
 
@@ -183,18 +196,18 @@ def tile_memory_pa_s_kernel(tc, memory, key, strength, sharpen, out):
                 cols = slice((t % TILES_PER_BANK) * P, (t % TILES_PER_BANK + 1) * P)
                 nc.tensor.transpose(sim[t // TILES_PER_BANK][:, cols], sim_t_of[r][:, i, :], identity[:])
 
-        z = keep.tile([P, SLOTS], F32)
-        z_max = keep.tile([P, OUT_BANKS], F32)
+        neg_z = keep.tile([P, SLOTS], F32)
+        neg_z_min = keep.tile([P, OUT_BANKS], F32)
 
         def scale_bank(h):
             nc.vector.tensor_scalar(
-                out=z[:, h * BANK : (h + 1) * BANK],
+                out=neg_z[:, h * BANK : (h + 1) * BANK],
                 in0=sim[h][:],
-                scalar1=gain[:, 0:1],
-                scalar2=None,
+                scalar1=neg_gain[:, 0:1],
+                scalar2=None if h == 0 else neg_z_min[:, h - 1 : h],
                 op0=ALU.mult,
-                op1=ALU.max,
-                accum_out=z_max[:, h : h + 1],
+                op1=ALU.min,
+                accum_out=neg_z_min[:, h : h + 1],
             )
 
         key_bank = pair_banks.tile([P, PAIR_BLOCKS, P], F32, name="pair_bank")
@@ -225,23 +238,22 @@ def tile_memory_pa_s_kernel(tc, memory, key, strength, sharpen, out):
             if s >= 2 and (s - 1) % rounds_per_bank == 0:
                 scale_bank((s - 2) // rounds_per_bank)
 
-        neg_max = keep.tile([P, 1], F32)
-        nc.vector.tensor_reduce(out=neg_max[:], in_=z_max[:], axis=AXIS.X, op=ALU.max, negate=True)
+        neg_max = neg_z_min[:, OUT_BANKS - 1 : OUT_BANKS]
         e_unread = keep.tile([P, SLOTS], BF16)
         e_sum = keep.tile([P, 1], F32)
         nc.scalar.activation(
-            out=e_unread[:], in_=z[:], func=ACT.Exp, bias=neg_max[:, 0:1], scale=1.0, accum_out=e_sum[:]
+            out=e_unread[:], in_=neg_z[:], func=ACT.Exp, bias=neg_max, scale=-1.0, accum_out=e_sum[:]
         )
         neg_max_sharp = keep.tile([P, 1], F32)
-        nc.vector.tensor_tensor(out=neg_max_sharp[:], in0=neg_max[:], in1=sharpen_f32[:], op=ALU.mult)
+        nc.vector.tensor_tensor(out=neg_max_sharp[:], in0=neg_max, in1=sharpen_f32[:], op=ALU.mult)
         v = keep.tile([P, SLOTS], F32)
         v_sum = keep.tile([P, 1], F32)
         nc.scalar.activation(
             out=v[:],
-            in_=z[:],
+            in_=neg_z[:],
             func=ACT.Exp,
             bias=neg_max_sharp[:, 0:1],
-            scale=sharpen_f32[:, 0:1],
+            scale=neg_sharpen[:, 0:1],
             accum_out=v_sum[:],
         )
         e_sum_sharp = keep.tile([P, 1], F32)

@@ -59,12 +59,13 @@ def tile_memory_pa_s_kernel(tc, memory, key, strength, sharpen, out):
         ctx.enter_context(tc.manual_schedule())
 
         key_rows = keep.tile([P, FEATURES], BF16)
-        nc.sync.dma_start(out=key_rows[:], in_=key)
         mem_rows = []
         for t in range(SLOT_TILES):
             rows = keep.tile([P, FEATURES], BF16, name="mem_rows%d" % t)
             nc.sync.dma_start(out=rows[:], in_=mem[t * P : (t + 1) * P, :])
             mem_rows.append(rows)
+            if t == 0:
+                nc.sync.dma_start(out=key_rows[:], in_=key)
 
         identity = keep.tile([P, P], F32)
         masks.make_identity(nc, identity[:])
@@ -78,36 +79,15 @@ def tile_memory_pa_s_kernel(tc, memory, key, strength, sharpen, out):
         nc.vector.memset(zero_col[:], 0.0)
         warm_col = keep.tile([P, 1], F32)
         nc.scalar.activation(out=warm_col[:], in_=zero_col[:], func=ACT.Exp)
-
-        squares = keep.tile([P, 1 + SLOT_TILES, FEATURES], BF16)
-        key_sumsq = keep.tile([P, 1], F32)
-        nc.scalar.activation(
-            out=squares[:, SLOT_TILES, :], in_=key_rows[:], func=ACT.Square, accum_out=key_sumsq[:]
-        )
-        key_inv_norm = keep.tile([P, 1], F32)
-        nc.gpsimd.tensor_tensor(
-            out=key_inv_norm[:], in0=key_sumsq[:], in1=minus_half[:, 0:1], op=ALU.pow
-        )
-        key_inv_clamped = keep.tile([P, 1], F32)
-        nc.gpsimd.tensor_scalar(
-            out=key_inv_clamped[:],
-            in0=key_inv_norm[:],
-            scalar1=1.0 / EPS,
-            scalar2=-1.0,
-            op0=ALU.min,
-            op1=ALU.mult,
-        )
-        neg_gain = keep.tile([P, 1], F32)
-        nc.gpsimd.tensor_tensor(
-            out=neg_gain[:], in0=key_inv_clamped[:], in1=strength_col[:], op=ALU.mult
-        )
         sharpen_f32 = keep.tile([P, 1], F32)
         nc.gpsimd.tensor_copy(out=sharpen_f32[:], in_=sharpen_col[:])
-        neg_sharpen = keep.tile([P, 1], F32)
-        nc.gpsimd.tensor_scalar(
-            out=neg_sharpen[:], in0=sharpen_col[:], scalar1=-1.0, scalar2=None, op0=ALU.mult
+        strengths = keep.tile([P, 2], F32)
+        nc.gpsimd.tensor_copy(out=strengths[:, 0:1], in_=strength_col[:])
+        nc.gpsimd.tensor_tensor(
+            out=strengths[:, 1:2], in0=strength_col[:], in1=sharpen_col[:], op=ALU.mult
         )
 
+        squares = keep.tile([P, 1 + SLOT_TILES, FEATURES], BF16)
         mem_sumsq = keep.tile([P, SLOT_TILES], F32)
         mem_inv_norm = keep.tile([P, SLOT_TILES], F32)
         for r in range(ROUNDS):
@@ -125,6 +105,14 @@ def tile_memory_pa_s_kernel(tc, memory, key, strength, sharpen, out):
                 in1=minus_half[:, tiles],
                 op=ALU.pow,
             )
+        key_sumsq = keep.tile([P, 1], F32)
+        nc.scalar.activation(
+            out=squares[:, SLOT_TILES, :], in_=key_rows[:], func=ACT.Square, accum_out=key_sumsq[:]
+        )
+        key_inv_norm = keep.tile([P, 1], F32)
+        nc.gpsimd.tensor_tensor(
+            out=key_inv_norm[:], in0=key_sumsq[:], in1=minus_half[:, 0:1], op=ALU.pow
+        )
 
         banks_of = {}
         grouped_of = {}
@@ -196,18 +184,18 @@ def tile_memory_pa_s_kernel(tc, memory, key, strength, sharpen, out):
                 cols = slice((t % TILES_PER_BANK) * P, (t % TILES_PER_BANK + 1) * P)
                 nc.tensor.transpose(sim[t // TILES_PER_BANK][:, cols], sim_t_of[r][:, i, :], identity[:])
 
-        neg_z = keep.tile([P, SLOTS], F32)
-        neg_z_min = keep.tile([P, OUT_BANKS], F32)
+        sim_rows = keep.tile([P, SLOTS], F32)
+        sim_max = keep.tile([P, OUT_BANKS], F32)
 
-        def scale_bank(h):
+        def copy_bank(h):
             nc.vector.tensor_scalar(
-                out=neg_z[:, h * BANK : (h + 1) * BANK],
+                out=sim_rows[:, h * BANK : (h + 1) * BANK],
                 in0=sim[h][:],
-                scalar1=neg_gain[:, 0:1],
-                scalar2=None if h == 0 else neg_z_min[:, h - 1 : h],
+                scalar1=1.0,
+                scalar2=None if h == 0 else sim_max[:, h - 1 : h],
                 op0=ALU.mult,
-                op1=ALU.min,
-                accum_out=neg_z_min[:, h : h + 1],
+                op1=ALU.max,
+                accum_out=sim_max[:, h : h + 1],
             )
 
         key_bank = pair_banks.tile([P, PAIR_BLOCKS, P], F32, name="pair_bank")
@@ -236,24 +224,44 @@ def tile_memory_pa_s_kernel(tc, memory, key, strength, sharpen, out):
                 normalise_round(s - 1)
                 transpose_back_round(s - 1)
             if s >= 2 and (s - 1) % rounds_per_bank == 0:
-                scale_bank((s - 2) // rounds_per_bank)
+                copy_bank((s - 2) // rounds_per_bank)
 
-        neg_max = neg_z_min[:, OUT_BANKS - 1 : OUT_BANKS]
+        gains = keep.tile([P, 2], F32)
+        nc.vector.scalar_tensor_tensor(
+            out=gains[:],
+            in0=key_inv_norm[:, 0:1].to_broadcast([P, 2]),
+            scalar=1.0 / EPS,
+            in1=strengths[:],
+            op0=ALU.min,
+            op1=ALU.mult,
+        )
+        neg_shifts = keep.tile([P, 2], F32)
+        nc.vector.tensor_scalar(
+            out=neg_shifts[:],
+            in0=gains[:],
+            scalar1=sim_max[:, OUT_BANKS - 1 : OUT_BANKS],
+            scalar2=-1.0,
+            op0=ALU.mult,
+            op1=ALU.mult,
+        )
         e_unread = keep.tile([P, SLOTS], BF16)
         e_sum = keep.tile([P, 1], F32)
         nc.scalar.activation(
-            out=e_unread[:], in_=neg_z[:], func=ACT.Exp, bias=neg_max, scale=-1.0, accum_out=e_sum[:]
+            out=e_unread[:],
+            in_=sim_rows[:],
+            func=ACT.Exp,
+            bias=neg_shifts[:, 0:1],
+            scale=gains[:, 0:1],
+            accum_out=e_sum[:],
         )
-        neg_max_sharp = keep.tile([P, 1], F32)
-        nc.vector.tensor_tensor(out=neg_max_sharp[:], in0=neg_max, in1=sharpen_f32[:], op=ALU.mult)
         v = keep.tile([P, SLOTS], F32)
         v_sum = keep.tile([P, 1], F32)
         nc.scalar.activation(
             out=v[:],
-            in_=neg_z[:],
+            in_=sim_rows[:],
             func=ACT.Exp,
-            bias=neg_max_sharp[:, 0:1],
-            scale=neg_sharpen[:, 0:1],
+            bias=neg_shifts[:, 1:2],
+            scale=gains[:, 1:2],
             accum_out=v_sum[:],
         )
         e_sum_sharp = keep.tile([P, 1], F32)

from contextlib import ExitStack

import concourse.masks as masks
import concourse.mybir as mybir

F32 = mybir.dt.float32
BF16 = mybir.dt.bfloat16
U32 = mybir.dt.uint32
U8 = mybir.dt.uint8
FP8X4 = mybir.dt.float8_e4m3fn_x4
ALU = mybir.AluOpType
ACT = mybir.ActivationFunctionType

P = 128
SLOTS = 1024
FEATURES = 1024
KEYS = 128
PACK = 4
K_PASS = P * PACK
PASSES = FEATURES // K_PASS
PAIRS = FEATURES // 2
PAIR_BLOCKS = PAIRS // P
HALVES = PAIR_BLOCKS // PASSES
TILE_WORDS = PASSES * P
SLOT_TILES = SLOTS // P
TILES_PER_ROUND = 2
ROUNDS = SLOT_TILES // TILES_PER_ROUND
BANK = 512
TILES_PER_BANK = BANK // P
OUT_BANKS = SLOTS // BANK
EPS = 1e-8
TINY = 1e-16

FLOPS = 2 * KEYS * SLOTS * FEATURES


def transpose_pairs(nc, bank, rows, identity):
    pairs = rows.bitcast(F32)
    for j in range(PAIR_BLOCKS):
        nc.tensor.transpose(bank[:, j, :], pairs[:, j * P : (j + 1) * P], identity)


def regroup(nc, grouped, bank):
    nc.vector.tensor_copy(
        out=grouped.bitcast(F32).rearrange("p (g r u) -> p g r u", g=PASSES, u=HALVES),
        in_=bank.rearrange("p (g u) r -> p g r u", u=HALVES),
    )


def tile_memory_pa_s_kernel(tc, memory, key, strength, sharpen, out):
    nc = tc.nc
    mem = memory.rearrange("n c h w -> n (c h w)")
    with ExitStack() as ctx:
        keep = ctx.enter_context(tc.tile_pool(name="keep", bufs=1))
        stage = ctx.enter_context(tc.tile_pool(name="stage", bufs=2))
        pair_banks = ctx.enter_context(tc.psum_pool(name="pair_banks", bufs=4))
        dot_banks = ctx.enter_context(tc.psum_pool(name="dot_banks", bufs=2))
        sim_banks = ctx.enter_context(tc.psum_pool(name="sim_banks", bufs=1))
        ctx.enter_context(tc.manual_schedule())

        key_rows = keep.tile([P, FEATURES], BF16)
        mem_rows = []
        for t in range(SLOT_TILES):
            rows = keep.tile([P, FEATURES], BF16, name="mem_rows%d" % t)
            nc.sync.dma_start(out=rows[:], in_=mem[t * P : (t + 1) * P, :])
            mem_rows.append(rows)
            if t == 0:
                nc.sync.dma_start(out=key_rows[:], in_=key)

        identity = keep.tile([P, P], F32)
        masks.make_identity(nc, identity[:])
        strength_col = keep.tile([P, 1], BF16)
        nc.gpsimd.dma_start(out=strength_col[:], in_=strength)
        sharpen_col = keep.tile([P, 1], BF16)
        nc.gpsimd.dma_start(out=sharpen_col[:], in_=sharpen)
        minus_half = keep.tile([P, SLOT_TILES], F32)
        nc.vector.memset(minus_half[:], -0.5)
        zero_col = keep.tile([P, 1], F32)
        nc.vector.memset(zero_col[:], 0.0)
        warm_col = keep.tile([P, 1], F32)
        nc.scalar.activation(out=warm_col[:], in_=zero_col[:], func=ACT.Exp)
        sharpen_f32 = keep.tile([P, 1], F32)
        nc.gpsimd.tensor_copy(out=sharpen_f32[:], in_=sharpen_col[:])
        strengths = keep.tile([P, 2], F32)
        nc.gpsimd.tensor_copy(out=strengths[:, 0:1], in_=strength_col[:])
        nc.gpsimd.tensor_tensor(
            out=strengths[:, 1:2], in0=strength_col[:], in1=sharpen_col[:], op=ALU.mult
        )

        squares = keep.tile([P, 1 + SLOT_TILES, FEATURES], BF16)
        mem_sumsq = keep.tile([P, SLOT_TILES], F32)
        mem_inv_norm = keep.tile([P, SLOT_TILES], F32)
        for r in range(ROUNDS):
            tiles = slice(r * TILES_PER_ROUND, (r + 1) * TILES_PER_ROUND)
            for t in range(r * TILES_PER_ROUND, (r + 1) * TILES_PER_ROUND):
                nc.scalar.activation(
                    out=squares[:, t, :],
                    in_=mem_rows[t][:],
                    func=ACT.Square,
                    accum_out=mem_sumsq[:, t : t + 1],
                )
            nc.gpsimd.tensor_tensor(
                out=mem_inv_norm[:, tiles],
                in0=mem_sumsq[:, tiles],
                in1=minus_half[:, tiles],
                op=ALU.pow,
            )
        key_sumsq = keep.tile([P, 1], F32)
        nc.scalar.activation(
            out=squares[:, SLOT_TILES, :], in_=key_rows[:], func=ACT.Square, accum_out=key_sumsq[:]
        )
        key_inv_norm = keep.tile([P, 1], F32)
        nc.gpsimd.tensor_tensor(
            out=key_inv_norm[:], in0=key_sumsq[:], in1=minus_half[:, 0:1], op=ALU.pow
        )

        banks_of = {}
        grouped_of = {}
        codes_of = {}
        scales_of = {}
        dot_of = {}
        sim_t_of = {}
        sim = [sim_banks.tile([P, BANK], F32, name="sim%d" % h) for h in range(OUT_BANKS)]

        def transpose_round(r):
            banks_of[r] = []
            for i in range(TILES_PER_ROUND):
                bank = pair_banks.tile([P, PAIR_BLOCKS, P], F32, name="pair_bank")
                transpose_pairs(nc, bank, mem_rows[r * TILES_PER_ROUND + i][:], identity[:])
                banks_of[r].append(bank)

        def regroup_round(r):
            grouped = stage.tile(
                [P, TILES_PER_ROUND, TILE_WORDS * PACK], BF16, name="grouped", align_bytes=64
            )
            for i in range(TILES_PER_ROUND):
                regroup(nc, grouped[:, i, :], banks_of[r][i][:])
            grouped_of[r] = grouped

        def quantise_round(r):
            codes = stage.tile([P, TILES_PER_ROUND * TILE_WORDS], U32, name="codes", align_bytes=64)
            scales = stage.tile([P, TILES_PER_ROUND * TILE_WORDS], U8, name="scales", align_bytes=64)
            nc.vector.quantize_mx(
                out=codes[:].bitcast(FP8X4),
                scales=scales[:],
                in_=grouped_of[r][:].rearrange("p i c -> p (i c)"),
            )
            codes_of[r] = codes
            scales_of[r] = scales

        def multiply_round(r):
            dot = dot_banks.tile([P, TILES_PER_ROUND, KEYS], F32, name="dot")
            for i in range(TILES_PER_ROUND):
                for g in range(PASSES):
                    slot_cols = slice((i * PASSES + g) * P, (i * PASSES + g + 1) * P)
                    key_cols = slice(g * KEYS, (g + 1) * KEYS)
                    nc.tensor.matmul_mx(
                        out=dot[:, i, :],
                        lhsT=codes_of[r][:, slot_cols].bitcast(FP8X4),
                        lhsT_scale=scales_of[r][:, slot_cols],
                        rhs=key_codes[:, key_cols].bitcast(FP8X4),
                        rhs_scale=key_scales[:, key_cols],
                        start=(g == 0),
                        stop=(g == PASSES - 1),
                    )
            dot_of[r] = dot

        def normalise_round(r):
            tiles = slice(r * TILES_PER_ROUND, (r + 1) * TILES_PER_ROUND)
            sim_t = stage.tile([P, TILES_PER_ROUND, KEYS], F32, name="sim_t")
            nc.vector.scalar_tensor_tensor(
                out=sim_t[:],
                in0=mem_inv_norm[:, tiles].unsqueeze(2).to_broadcast([P, TILES_PER_ROUND, KEYS]),
                scalar=1.0 / EPS,
                in1=dot_of[r][:],
                op0=ALU.min,
                op1=ALU.mult,
            )
            sim_t_of[r] = sim_t

        def transpose_back_round(r):
            for i in range(TILES_PER_ROUND):
                t = r * TILES_PER_ROUND + i
                cols = slice((t % TILES_PER_BANK) * P, (t % TILES_PER_BANK + 1) * P)
                nc.tensor.transpose(sim[t // TILES_PER_BANK][:, cols], sim_t_of[r][:, i, :], identity[:])

        sim_rows = keep.tile([P, SLOTS], F32)
        sim_max = keep.tile([P, OUT_BANKS], F32)

        def copy_bank(h):
            nc.vector.tensor_scalar(
                out=sim_rows[:, h * BANK : (h + 1) * BANK],
                in0=sim[h][:],
                scalar1=1.0,
                scalar2=None if h == 0 else sim_max[:, h - 1 : h],
                op0=ALU.mult,
                op1=ALU.max,
                accum_out=sim_max[:, h : h + 1],
            )

        key_bank = pair_banks.tile([P, PAIR_BLOCKS, P], F32, name="pair_bank")
        transpose_pairs(nc, key_bank, key_rows[:], identity[:])
        key_grouped = keep.tile([P, TILE_WORDS * PACK], BF16, align_bytes=64)
        regroup(nc, key_grouped[:], key_bank[:])
        transpose_round(0)
        regroup_round(0)
        key_codes = keep.tile([P, TILE_WORDS], U32, align_bytes=64)
        key_scales = keep.tile([P, TILE_WORDS], U8, align_bytes=64)
        nc.vector.quantize_mx(
            out=key_codes[:].bitcast(FP8X4), scales=key_scales[:], in_=key_grouped[:]
        )
        transpose_round(1)

        rounds_per_bank = TILES_PER_BANK // TILES_PER_ROUND
        for s in range(ROUNDS + 2):
            if s + 2 < ROUNDS:
                transpose_round(s + 2)
            if s + 1 < ROUNDS:
                regroup_round(s + 1)
            if s < ROUNDS:
                quantise_round(s)
                multiply_round(s)
            if 1 <= s <= ROUNDS:
                normalise_round(s - 1)
                transpose_back_round(s - 1)
            if s >= 2 and (s - 1) % rounds_per_bank == 0:
                copy_bank((s - 2) // rounds_per_bank)

        gains = keep.tile([P, 2], F32)
        nc.vector.scalar_tensor_tensor(
            out=gains[:],
            in0=key_inv_norm[:, 0:1].to_broadcast([P, 2]),
            scalar=1.0 / EPS,
            in1=strengths[:],
            op0=ALU.min,
            op1=ALU.mult,
        )
        neg_shifts = keep.tile([P, 2], F32)
        nc.vector.tensor_scalar(
            out=neg_shifts[:],
            in0=gains[:],
            scalar1=sim_max[:, OUT_BANKS - 1 : OUT_BANKS],
            scalar2=-1.0,
            op0=ALU.mult,
            op1=ALU.mult,
        )
        e_unread = keep.tile([P, SLOTS], BF16)
        e_sum = keep.tile([P, 1], F32)
        nc.scalar.activation(
            out=e_unread[:],
            in_=sim_rows[:],
            func=ACT.Exp,
            bias=neg_shifts[:, 0:1],
            scale=gains[:, 0:1],
            accum_out=e_sum[:],
        )
        v = keep.tile([P, SLOTS], F32)
        v_sum = keep.tile([P, 1], F32)
        nc.scalar.activation(
            out=v[:],
            in_=sim_rows[:],
            func=ACT.Exp,
            bias=neg_shifts[:, 1:2],
            scale=gains[:, 1:2],
            accum_out=v_sum[:],
        )
        e_sum_sharp = keep.tile([P, 1], F32)
        nc.gpsimd.tensor_tensor(out=e_sum_sharp[:], in0=e_sum[:], in1=sharpen_f32[:], op=ALU.pow)
        denominator = keep.tile([P, 1], F32)
        nc.vector.tensor_scalar(
            out=denominator[:],
            in0=e_sum_sharp[:],
            scalar1=TINY,
            scalar2=v_sum[:, 0:1],
            op0=ALU.mult,
            op1=ALU.add,
        )
        inv_denominator = keep.tile([P, 1], F32)
        nc.vector.reciprocal(out=inv_denominator[:], in_=denominator[:])
        w = keep.tile([P, SLOTS], F32)
        for h in range(OUT_BANKS):
            cols = slice(h * BANK, (h + 1) * BANK)
            nc.vector.tensor_scalar(
                out=w[:, cols], in0=v[:, cols], scalar1=inv_denominator[:, 0:1], scalar2=None, op0=ALU.mult
            )
            nc.sync.dma_start(out=out[:, cols], in_=w[:, cols])
